import numpy as np
import ml_dtypes


def mxq(x, axis, fmt="e4m3"):
    dtype, down = {"e4m3": (ml_dtypes.float8_e4m3fn, 7), "e5m2": (ml_dtypes.float8_e5m2, 14)}[fmt]
    v = np.moveaxis(np.asarray(x, np.float32).astype(ml_dtypes.bfloat16).astype(np.float64), axis, -1)
    blocks = v.reshape(v.shape[:-1] + (-1, 32))
    amax = np.abs(blocks).max(-1, keepdims=True)
    byte = np.maximum(np.where(amax > 0, np.frexp(amax)[1] - 1 + 127, 0) - down, 1)
    scale = np.exp2(byte - 127.0)
    codes = (blocks / scale).astype(np.float32).astype(dtype).astype(np.float64)
    return np.moveaxis((codes * scale).reshape(v.shape), -1, axis)


WIDE = False


def mx_kscale(k):
    if not WIDE:
        return np.ones(k)
    levels = np.array([30, -30])
    if k % 512:
        return np.exp2(np.random.permutation(np.resize(levels, k // 32))).repeat(32)
    a = np.empty((k // 512, 16))
    for p in range(k // 512):
        a[p, :8] = np.random.permutation(np.resize(levels, 8))
        for g in range(8):
            far = levels[np.abs(levels - a[p, g]) >= 10]
            a[p, g + 8] = far[np.random.randint(len(far))]
    return np.exp2(a.ravel()).repeat(32)


BF16 = ml_dtypes.bfloat16


def bf(x):
    return np.asarray(x, np.float32).astype(BF16)


def f64(x):
    return np.asarray(x).astype(np.float64)


B, C, H, W, K, HID, LAT = 4, 512, 16, 16, 8, 512, 32
REDUCTION = -0.1
CLAMP = 500.0
HOT = 1.2 * CLAMP / (-REDUCTION * C * np.sqrt(2.0 / np.pi))


def setup_inputs():
    s = mx_kscale(HID)
    amp = np.where(np.random.random((B, 1, H, W)) < 0.125, HOT, 1.0)
    return {"d": bf(np.tanh(np.random.standard_normal((K, B, HID, H, W))) * s[:, None, None]),
            "W_dec": bf(np.random.standard_normal((K, C, HID)) * 1.1 / np.sqrt(HID) / s),
            "x": bf(np.random.standard_normal((B, C, H, W)) * amp)}


def reference(d, W_dec, x):
    xf = f64(x)
    wq = mxq(f64(W_dec), 2, "e5m2")
    dq = mxq(f64(d), 2, "e5m2")
    recon = (wq[:, None] @ dq.reshape(K, B, HID, H * W)).reshape(K, B, C, H, W)
    err = np.sum(np.abs(recon - xf[None]), axis=2) * REDUCTION
    logits = np.swapaxes(np.clip(err, -CLAMP, CLAMP), 0, 1)
    e = np.exp(logits - logits.max(axis=1, keepdims=True))
    p = e / e.sum(axis=1, keepdims=True)
    error = np.mean(logits, axis=(2, 3))
    return p, error, np.swapaxes(recon, 0, 1)

@@ -1,0 +1,299 @@
+from contextlib import ExitStack
+
+import concourse.mybir as mybir
+from concourse.masks import make_identity
+
+B, C, HW, K, HID = 4, 512, 256, 8, 512
+REDUCTION = -0.1
+CLAMP = 500.0
+FLOPS = 2 * K * C * HID * B * HW
+
+F32 = mybir.dt.float32
+BF16 = mybir.dt.bfloat16
+U32 = mybir.dt.uint32
+U8 = mybir.dt.uint8
+E5M2X4 = mybir.dt.float8_e5m2_x4
+ALU = mybir.AluOpType
+ACT = mybir.ActivationFunctionType
+AX = mybir.AxisListType
+
+P = 128
+PACK = 4
+BANK = 512
+PAIR = 2
+STEPS = K * B // PAIR
+PATCHES = PAIR * HW // P
+BY_MATMUL = (3,)
+
+
+def tile_cssrclassifier_pa_kernel(tc, d, W_dec, x, out_0, out_1, out_2):
+    nc = tc.nc
+    by_transpose = [q for q in range(PATCHES) if q not in BY_MATMUL]
+
+    with ExitStack() as ctx:
+        keep = ctx.enter_context(tc.tile_pool(name="keep", bufs=1))
+        loads = ctx.enter_context(tc.tile_pool(name="loads", bufs=4))
+        work = ctx.enter_context(tc.tile_pool(name="work", bufs=3))
+        psum = ctx.enter_context(tc.psum_pool(name="psum", bufs=8))
+        ctx.enter_context(tc.manual_schedule())
+
+        ident = keep.tile([P, P], F32, name="ident")
+        make_identity(nc, ident[:])
+        selector = keep.tile([P, P + B - 1], F32, name="selector")
+        nc.gpsimd.memset(selector[:], 0.0)
+        nc.gpsimd.memset(selector[:, B - 1 : B], 1.0 / HW)
+        sums = keep.tile([P, B * 2, K], F32, name="sums")
+
+        d_raw, d_grouped, d_codes, d_scales = {}, {}, {}, {}
+        w_raw, w_bank, w_grouped, w_codes, w_scales = {}, {}, {}, {}, {}
+        x_raw, neg_x, neg_xt, recon = {}, {}, {}, {}
+
+        def bank():
+            return psum.tile([P, BANK], F32, name="bank")
+
+        def load_d(s):
+            k, h = divmod(s, 2)
+            d_raw[s] = loads.tile([P, PAIR, PACK, HW], BF16, name="d_raw")
+            nc.sync.dma_start(
+                out=d_raw[s][:],
+                in_=d[k, PAIR * h : PAIR * (h + 1)].rearrange("b (p j) h w -> p b j (h w)", j=PACK),
+            )
+
+        def load_w(i):
+            k, half = divmod(i, 2)
+            w_raw[i] = loads.tile([P, 2, HID], BF16, name="w_raw")
+            nc.sync.dma_start(
+                out=w_raw[i][:],
+                in_=W_dec[k].rearrange("(m t) j -> m t j", t=PACK)[:, 2 * half : 2 * half + 2, :],
+            )
+
+        def load_x(h):
+            x_raw[h] = keep.tile([P, PAIR, PACK * HW], BF16, name="x_raw%d" % h)
+            nc.sync.dma_start(
+                out=x_raw[h][:],
+                in_=x[PAIR * h : PAIR * (h + 1)].rearrange("b (m t) h w -> m b (t h w)", t=PACK),
+            )
+
+        def negate_x(h):
+            neg_x[h] = keep.tile([P, PAIR, PACK, HW], F32, name="neg_x%d" % h)
+            nc.scalar.mul(
+                out=neg_x[h][:].rearrange("p b t n -> p (b t n)"),
+                in_=x_raw[h][:].rearrange("p b n -> p (b n)"),
+                mul=-1.0,
+            )
+
+        def patch(tile, q, t):
+            b, hh = divmod(q, 2)
+            return tile[:, b, t, hh * P : (hh + 1) * P]
+
+        def transpose_x(h, q):
+            acc = bank()
+            for t in range(PACK):
+                nc.tensor.transpose(acc[:, t * P : (t + 1) * P], patch(neg_x[h], q, t), ident[:])
+            neg_xt[h, q] = keep.tile([P, C], F32, name="neg_xt%d_%d" % (h, q))
+            nc.vector.tensor_copy(out=neg_xt[h, q][:], in_=acc[:])
+
+        def interleave_d(s):
+            d_grouped[s] = work.tile([P, PAIR, HW, PACK], BF16, name="d_grouped", align_bytes=64)
+            nc.vector.tensor_copy(out=d_grouped[s][:], in_=d_raw[s][:].rearrange("p b j n -> p b n j"))
+
+        def quantize_d(s):
+            d_codes[s] = work.tile([P, PAIR * HW], U32, name="d_codes", align_bytes=64)
+            d_scales[s] = work.tile([P, PAIR * HW], U8, name="d_scales", align_bytes=64)
+            nc.vector.quantize_mx(
+                out=d_codes[s][:].bitcast(E5M2X4),
+                scales=d_scales[s][:],
+                in_=d_grouped[s][:].rearrange("p b n j -> p (b n j)"),
+            )
+
+        def transpose_w(i):
+            w_bank[i] = bank()
+            view = w_bank[i][:].rearrange("p (t u m) -> p t u m", t=2, u=2)
+            for t in range(2):
+                words = w_raw[i][:, t, :].bitcast(F32)
+                for u in range(2):
+                    nc.tensor.transpose(view[:, t, u, :], words[:, u : HID // 2 : 2], ident[:])
+
+        def copy_w(i, engine_copy):
+            w_grouped[i] = work.tile([P, 2 * P * PACK], BF16, name="w_grouped", align_bytes=64)
+            engine_copy(
+                out=w_grouped[i][:].bitcast(F32).rearrange("p (t m u) -> p t m u", t=2, u=2),
+                in_=w_bank[i][:].rearrange("p (t u m) -> p t m u", t=2, u=2),
+            )
+
+        def quantize_w(i):
+            k, half = divmod(i, 2)
+            if half == 0:
+                w_codes[k] = work.tile([P, C], U32, name="w_codes", align_bytes=64)
+                w_scales[k] = work.tile([P, C], U8, name="w_scales", align_bytes=64)
+            cols = slice(half * 2 * P, (half + 1) * 2 * P)
+            nc.vector.quantize_mx(
+                out=w_codes[k][:, cols].bitcast(E5M2X4),
+                scales=w_scales[k][:, cols],
+                in_=w_grouped[i][:],
+            )
+
+        def decode(s, t):
+            k = s // 2
+            acc = bank()
+            cols = slice(t * P, (t + 1) * P)
+            nc.tensor.matmul_mx(
+                out=acc[:],
+                lhsT=w_codes[k][:, cols].bitcast(E5M2X4),
+                lhsT_scale=w_scales[k][:, cols],
+                rhs=d_codes[s][:].bitcast(E5M2X4),
+                rhs_scale=d_scales[s][:],
+                start=True,
+                stop=True,
+            )
+            return acc
+
+        def decode_transposed(s, q):
+            k = s // 2
+            acc = bank()
+            cols = slice(q * P, (q + 1) * P)
+            nc.tensor.matmul_mx(
+                out=acc[:],
+                lhsT=d_codes[s][:, cols].bitcast(E5M2X4),
+                lhsT_scale=d_scales[s][:, cols],
+                rhs=w_codes[k][:].bitcast(E5M2X4),
+                rhs_scale=w_scales[k][:],
+                start=True,
+                stop=True,
+            )
+            return acc
+
+        def abs_sum(s, q, diff):
+            k, h = divmod(s, 2)
+            magnitude = work.tile([P, C], F32, name="magnitude")
+            nc.scalar.activation(
+                out=magnitude[:],
+                in_=diff[:],
+                func=ACT.Abs,
+                accum_out=sums[:, h * PATCHES + q, k : k + 1],
+            )
+
+        def difference_by_transposes(s, q):
+            h = s % 2
+            acc = bank()
+            for t in range(PACK):
+                cols = acc[:, t * P : (t + 1) * P]
+                nc.tensor.matmul(cols, lhsT=patch(neg_x[h], q, t), rhs=ident[:], start=True, stop=False, is_transpose=True)
+                nc.tensor.matmul(cols, lhsT=patch(recon[s], q, t), rhs=ident[:], start=False, stop=True, is_transpose=True)
+            return acc
+
+        def store_recon(s):
+            k, h = divmod(s, 2)
+            nc.sync.dma_start(
+                out=out_2[PAIR * h : PAIR * (h + 1), k].rearrange("b (m t) h w -> m b (t h w)", t=PACK),
+                in_=recon[s][:].rearrange("p b t n -> p b (t n)"),
+            )
+
+        load_w(0)
+        load_d(0)
+        load_w(1)
+        load_x(0)
+        load_d(1)
+        load_w(2)
+        load_x(1)
+        load_d(2)
+        load_w(3)
+        transpose_w(0)
+        transpose_w(1)
+        copy_w(0, nc.scalar.copy)
+        interleave_d(0)
+        copy_w(1, nc.scalar.copy)
+        quantize_w(0)
+        quantize_d(0)
+        quantize_w(1)
+        negate_x(0)
+        interleave_d(1)
+        transpose_w(2)
+
+        for s in range(STEPS + 1):
+            last = s == STEPS
+            h = s % 2
+            if s + 3 < STEPS:
+                load_d(s + 3)
+            if s + 4 < STEPS:
+                load_w(s + 4)
+            if s + 2 < STEPS:
+                copy_w(s + 2, nc.vector.tensor_copy)
+            if s + 1 < STEPS:
+                quantize_d(s + 1)
+            if s + 2 < STEPS:
+                quantize_w(s + 2)
+            diffs = []
+            if not last:
+                recon[s] = loads.tile([P, PAIR, PACK, HW], F32, name="recon")
+                accs = [decode(s, t) for t in range(PACK)]
+                direct = [decode_transposed(s, q) for q in BY_MATMUL]
+                for t in range(PACK):
+                    engine_copy = nc.vector.tensor_copy if t == PACK - 1 else nc.scalar.copy
+                    engine_copy(out=recon[s][:, :, t, :], in_=accs[t][:].rearrange("p (b n) -> p b n", b=PAIR))
+                store_recon(s)
+                if s == 0:
+                    negate_x(1)
+                for q, acc in zip(BY_MATMUL, direct):
+                    if s < 2:
+                        transpose_x(h, q)
+                    diff = work.tile([P, C], F32, name="diff")
+                    nc.vector.tensor_tensor(out=diff[:], in0=acc[:], in1=neg_xt[h, q][:], op=ALU.add)
+                    diffs.append((q, diff))
+            for n, q in enumerate(by_transpose):
+                if s > 0:
+                    abs_sum(s - 1, q, difference_by_transposes(s - 1, q))
+                if n < len(diffs):
+                    abs_sum(s, *diffs[n])
+            if s + 2 < STEPS:
+                interleave_d(s + 2)
+            if s + 3 < STEPS:
+                transpose_w(s + 3)
+
+        units = B * 2
+        both = keep.tile([P, P], F32, name="both")
+        logits = both[:, units * K :]
+        logits3 = logits.rearrange("p (u k) -> p u k", k=K)
+        scaled = keep.tile([P, units * K], F32, name="scaled")
+        nc.vector.tensor_scalar(
+            out=scaled[:], in0=sums[:].rearrange("p u k -> p (u k)"),
+            scalar1=REDUCTION, scalar2=-CLAMP, op0=ALU.mult, op1=ALU.max,
+        )
+        nc.vector.tensor_scalar_min(out=logits, in0=scaled[:], scalar1=CLAMP)
+        top = keep.tile([P, units], F32, name="top")
+        nc.vector.tensor_reduce(out=top[:], in_=logits3, axis=AX.X, op=ALU.max)
+        shifted = keep.tile([P, units, K], F32, name="shifted")
+        nc.vector.tensor_tensor(
+            out=shifted[:], in0=logits3, in1=top[:].unsqueeze(2).to_broadcast([P, units, K]), op=ALU.subtract
+        )
+        pooled = bank()
+        for b in range(B):
+            nc.tensor.matmul(
+                pooled[:, : 2 * K],
+                lhsT=selector[:, B - 1 - b : B - 1 - b + P],
+                rhs=logits[:, b * 2 * K : (b + 1) * 2 * K],
+                start=(b == 0),
+                stop=(b == B - 1),
+            )
+        powers = keep.tile([P, units, K], F32, name="powers")
+        nc.scalar.activation(out=powers[:], in_=shifted[:], func=ACT.Exp)
+        error = keep.tile([32, K], F32, name="error")
+        nc.vector.tensor_reduce(
+            out=error[:], in_=pooled[:32, : 2 * K].rearrange("p (h k) -> p k h", h=2), axis=AX.X, op=ALU.add
+        )
+        nc.sync.dma_start(out=out_1, in_=error[:B, :])
+        total = keep.tile([P, units], F32, name="total")
+        nc.vector.tensor_reduce(out=total[:], in_=powers[:], axis=AX.X, op=ALU.add)
+        inverse = keep.tile([P, units], F32, name="inverse")
+        nc.vector.reciprocal(out=inverse[:], in_=total[:])
+        nc.vector.tensor_tensor(
+            out=both[:, : units * K].rearrange("p (b k h) -> p b h k", b=B, h=2),
+            in0=powers[:].rearrange("p (b h) k -> p b h k", h=2),
+            in1=inverse[:].rearrange("p (b h) -> p b h", h=2).unsqueeze(3).to_broadcast([P, B, 2, K]),
+            op=ALU.mult,
+        )
+        flipped = bank()
+        nc.tensor.transpose(flipped[:, :P], both[:], ident[:])
+        rows = keep.tile([units * K, P], F32, name="rows")
+        nc.scalar.copy(out=rows[:], in_=flipped[: units * K, :P])
+        nc.sync.dma_start(out=out_0.rearrange("b k (g r) w -> (b k g) (r w)", g=2), in_=rows[:])

@@ -41,7 +41,7 @@ def tile_cssrclassifier_pa_kernel(tc, d, W_dec, x, out_0, out_1, out_2):
         make_identity(nc, ident[:])
         selector = keep.tile([P, P + B - 1], F32, name="selector")
         nc.gpsimd.memset(selector[:], 0.0)
-        nc.gpsimd.memset(selector[:, B - 1 : B], 1.0 / HW)
+        nc.gpsimd.memset(selector[:, B - 1 : B], -1.0 / HW)
         sums = keep.tile([P, B * 2, K], F32, name="sums")
 
         d_raw, d_grouped, d_codes, d_scales = {}, {}, {}, {}
@@ -51,21 +51,18 @@ def tile_cssrclassifier_pa_kernel(tc, d, W_dec, x, out_0, out_1, out_2):
         def bank():
             return psum.tile([P, BANK], F32, name="bank")
 
-        def load_d(s):
+        def load_d(s, images=slice(0, PAIR)):
             k, h = divmod(s, 2)
-            d_raw[s] = loads.tile([P, PAIR, PACK, HW], BF16, name="d_raw")
-            nc.sync.dma_start(
-                out=d_raw[s][:],
-                in_=d[k, PAIR * h : PAIR * (h + 1)].rearrange("b (p j) h w -> p b j (h w)", j=PACK),
-            )
+            if images.start == 0:
+                d_raw[s] = loads.tile([P, PAIR, PACK, HW], BF16, name="d_raw", bufs=6)
+            src = d[k, PAIR * h : PAIR * (h + 1)].rearrange("b (p j) h w -> p b j (h w)", j=PACK)
+            nc.sync.dma_start(out=d_raw[s][:, images], in_=src[:, images])
 
-        def load_w(i):
-            k, half = divmod(i, 2)
-            w_raw[i] = loads.tile([P, 2, HID], BF16, name="w_raw")
-            nc.sync.dma_start(
-                out=w_raw[i][:],
-                in_=W_dec[k].rearrange("(m t) j -> m t j", t=PACK)[:, 2 * half : 2 * half + 2, :],
-            )
+        def load_w(k, slots=slice(0, PACK)):
+            if slots.start == 0:
+                w_raw[k] = loads.tile([P, PACK, HID], BF16, name="w_raw")
+            src = W_dec[k].rearrange("(m t) j -> m t j", t=PACK)
+            nc.sync.dma_start(out=w_raw[k][:, slots], in_=src[:, slots])
 
         def load_x(h):
             x_raw[h] = keep.tile([P, PAIR, PACK * HW], BF16, name="x_raw%d" % h)
@@ -76,10 +73,10 @@ def tile_cssrclassifier_pa_kernel(tc, d, W_dec, x, out_0, out_1, out_2):
 
         def negate_x(h):
             neg_x[h] = keep.tile([P, PAIR, PACK, HW], F32, name="neg_x%d" % h)
-            nc.scalar.mul(
+            nc.vector.tensor_scalar_mul(
                 out=neg_x[h][:].rearrange("p b t n -> p (b t n)"),
-                in_=x_raw[h][:].rearrange("p b n -> p (b n)"),
-                mul=-1.0,
+                in0=x_raw[h][:].rearrange("p b n -> p (b n)"),
+                scalar1=-1.0,
             )
 
         def patch(tile, q, t):
@@ -91,15 +88,19 @@ def tile_cssrclassifier_pa_kernel(tc, d, W_dec, x, out_0, out_1, out_2):
             for t in range(PACK):
                 nc.tensor.transpose(acc[:, t * P : (t + 1) * P], patch(neg_x[h], q, t), ident[:])
             neg_xt[h, q] = keep.tile([P, C], F32, name="neg_xt%d_%d" % (h, q))
-            nc.vector.tensor_copy(out=neg_xt[h, q][:], in_=acc[:])
+            nc.scalar.copy(out=neg_xt[h, q][:], in_=acc[:])
 
-        def interleave_d(s):
-            d_grouped[s] = work.tile([P, PAIR, HW, PACK], BF16, name="d_grouped", align_bytes=64)
-            nc.vector.tensor_copy(out=d_grouped[s][:], in_=d_raw[s][:].rearrange("p b j n -> p b n j"))
+        def interleave_d(s, images=slice(0, PAIR)):
+            if images.start == 0:
+                d_grouped[s] = work.tile([P, PAIR, HW, PACK], BF16, name="d_grouped", align_bytes=64)
+            nc.vector.tensor_copy(
+                out=d_grouped[s][:, images].rearrange("p b (c i) j -> p b c j i", i=4),
+                in_=d_raw[s][:, images].rearrange("p b j (c i) -> p b c j i", i=4),
+            )
 
         def quantize_d(s):
-            d_codes[s] = work.tile([P, PAIR * HW], U32, name="d_codes", align_bytes=64)
-            d_scales[s] = work.tile([P, PAIR * HW], U8, name="d_scales", align_bytes=64)
+            d_codes[s] = loads.tile([P, PAIR * HW], U32, name="d_codes", align_bytes=64)
+            d_scales[s] = loads.tile([P, PAIR * HW], U8, name="d_scales", align_bytes=64)
             nc.vector.quantize_mx(
                 out=d_codes[s][:].bitcast(E5M2X4),
                 scales=d_scales[s][:],
@@ -110,7 +111,7 @@ def tile_cssrclassifier_pa_kernel(tc, d, W_dec, x, out_0, out_1, out_2):
             w_bank[i] = bank()
             view = w_bank[i][:].rearrange("p (t u m) -> p t u m", t=2, u=2)
             for t in range(2):
-                words = w_raw[i][:, t, :].bitcast(F32)
+                words = w_raw[i // 2][:, 2 * (i % 2) + t, :].bitcast(F32)
                 for u in range(2):
                     nc.tensor.transpose(view[:, t, u, :], words[:, u : HID // 2 : 2], ident[:])
 
@@ -170,6 +171,7 @@ def tile_cssrclassifier_pa_kernel(tc, d, W_dec, x, out_0, out_1, out_2):
                 out=magnitude[:],
                 in_=diff[:],
                 func=ACT.Abs,
+                scale=REDUCTION,
                 accum_out=sums[:, h * PATCHES + q, k : k + 1],
             )
 
@@ -189,47 +191,56 @@ def tile_cssrclassifier_pa_kernel(tc, d, W_dec, x, out_0, out_1, out_2):
                 in_=recon[s][:].rearrange("p b t n -> p b (t n)"),
             )
 
-        load_w(0)
-        load_d(0)
-        load_w(1)
-        load_x(0)
+        def vector_banks(s):
+            if s < 2:
+                return 0
+            if s + 2 >= STEPS:
+                return PACK
+            return 1 + s % 2
+
+        load_w(0, slice(0, 2))
+        load_d(0, slice(0, 1))
+        load_d(0, slice(1, 2))
+        load_w(0, slice(2, 4))
         load_d(1)
-        load_w(2)
-        load_x(1)
+        load_x(0)
+        load_w(1)
         load_d(2)
-        load_w(3)
+        load_x(1)
+        load_d(3)
+        load_d(4)
         transpose_w(0)
         transpose_w(1)
+        interleave_d(0, slice(0, 1))
+        interleave_d(0, slice(1, 2))
         copy_w(0, nc.scalar.copy)
-        interleave_d(0)
         copy_w(1, nc.scalar.copy)
         quantize_w(0)
         quantize_d(0)
         quantize_w(1)
-        negate_x(0)
         interleave_d(1)
-        transpose_w(2)
+        negate_x(0)
+        quantize_d(1)
 
         for s in range(STEPS + 1):
-            last = s == STEPS
             h = s % 2
-            if s + 3 < STEPS:
-                load_d(s + 3)
-            if s + 4 < STEPS:
-                load_w(s + 4)
+            if h == 0 and s + 4 < STEPS:
+                load_w(s // 2 + 2)
+            if s + 5 < STEPS:
+                load_d(s + 5)
             if s + 2 < STEPS:
-                copy_w(s + 2, nc.vector.tensor_copy)
-            if s + 1 < STEPS:
-                quantize_d(s + 1)
-            if s + 2 < STEPS:
-                quantize_w(s + 2)
+                interleave_d(s + 2)
             diffs = []
-            if not last:
-                recon[s] = loads.tile([P, PAIR, PACK, HW], F32, name="recon")
+            if s < STEPS:
+                recon[s] = loads.tile([P, PAIR, PACK, HW], F32, name="recon", bufs=6)
                 accs = [decode(s, t) for t in range(PACK)]
                 direct = [decode_transposed(s, q) for q in BY_MATMUL]
+                if s == 0:
+                    transpose_w(2)
+                if s + 2 < STEPS:
+                    copy_w(s + 2, nc.vector.tensor_copy)
                 for t in range(PACK):
-                    engine_copy = nc.vector.tensor_copy if t == PACK - 1 else nc.scalar.copy
+                    engine_copy = nc.vector.tensor_copy if t >= PACK - vector_banks(s) else nc.scalar.copy
                     engine_copy(out=recon[s][:, :, t, :], in_=accs[t][:].rearrange("p (b n) -> p b n", b=PAIR))
                 store_recon(s)
                 if s == 0:
@@ -240,13 +251,14 @@ def tile_cssrclassifier_pa_kernel(tc, d, W_dec, x, out_0, out_1, out_2):
                     diff = work.tile([P, C], F32, name="diff")
                     nc.vector.tensor_tensor(out=diff[:], in0=acc[:], in1=neg_xt[h, q][:], op=ALU.add)
                     diffs.append((q, diff))
-            for n, q in enumerate(by_transpose):
-                if s > 0:
-                    abs_sum(s - 1, q, difference_by_transposes(s - 1, q))
-                if n < len(diffs):
-                    abs_sum(s, *diffs[n])
             if s + 2 < STEPS:
-                interleave_d(s + 2)
+                quantize_w(s + 2)
+                quantize_d(s + 2)
+            if s > 0:
+                for q in by_transpose:
+                    abs_sum(s - 1, q, difference_by_transposes(s - 1, q))
+            for q, diff in diffs:
+                abs_sum(s, q, diff)
             if s + 3 < STEPS:
                 transpose_w(s + 3)
 
@@ -254,14 +266,12 @@ def tile_cssrclassifier_pa_kernel(tc, d, W_dec, x, out_0, out_1, out_2):
         both = keep.tile([P, P], F32, name="both")
         logits = both[:, units * K :]
         logits3 = logits.rearrange("p (u k) -> p u k", k=K)
-        scaled = keep.tile([P, units * K], F32, name="scaled")
         nc.vector.tensor_scalar(
-            out=scaled[:], in0=sums[:].rearrange("p u k -> p (u k)"),
-            scalar1=REDUCTION, scalar2=-CLAMP, op0=ALU.mult, op1=ALU.max,
+            out=logits, in0=sums[:].rearrange("p u k -> p (u k)"),
+            scalar1=-CLAMP, scalar2=CLAMP, op0=ALU.max, op1=ALU.min,
         )
-        nc.vector.tensor_scalar_min(out=logits, in0=scaled[:], scalar1=CLAMP)
         top = keep.tile([P, units], F32, name="top")
-        nc.vector.tensor_reduce(out=top[:], in_=logits3, axis=AX.X, op=ALU.max)
+        nc.vector.tensor_reduce(out=top[:], in_=logits3, axis=AX.X, op=ALU.min)
         shifted = keep.tile([P, units, K], F32, name="shifted")
         nc.vector.tensor_tensor(
             out=shifted[:], in0=logits3, in1=top[:].unsqueeze(2).to_broadcast([P, units, K]), op=ALU.subtract
@@ -276,7 +286,7 @@ def tile_cssrclassifier_pa_kernel(tc, d, W_dec, x, out_0, out_1, out_2):
                 stop=(b == B - 1),
             )
         powers = keep.tile([P, units, K], F32, name="powers")
-        nc.scalar.activation(out=powers[:], in_=shifted[:], func=ACT.Exp)
+        nc.scalar.activation(out=powers[:], in_=shifted[:], func=ACT.Exp, scale=-1.0)
         error = keep.tile([32, K], F32, name="error")
         nc.vector.tensor_reduce(
             out=error[:], in_=pooled[:32, : 2 * K].rearrange("p (h k) -> p k h", h=2), axis=AX.X, op=ALU.add

@@ -23,12 +23,10 @@ BANK = 512
 PAIR = 2
 STEPS = K * B // PAIR
 PATCHES = PAIR * HW // P
-BY_MATMUL = (3,)
 
 
 def tile_cssrclassifier_pa_kernel(tc, d, W_dec, x, out_0, out_1, out_2):
     nc = tc.nc
-    by_transpose = [q for q in range(PATCHES) if q not in BY_MATMUL]
 
     with ExitStack() as ctx:
         keep = ctx.enter_context(tc.tile_pool(name="keep", bufs=1))
@@ -39,6 +37,8 @@ def tile_cssrclassifier_pa_kernel(tc, d, W_dec, x, out_0, out_1, out_2):
 
         ident = keep.tile([P, P], F32, name="ident")
         make_identity(nc, ident[:])
+        ident_bf16 = keep.tile([P, P], BF16, name="ident_bf16")
+        make_identity(nc, ident_bf16[:])
         selector = keep.tile([P, P + B - 1], F32, name="selector")
         nc.gpsimd.memset(selector[:], 0.0)
         nc.gpsimd.memset(selector[:, B - 1 : B], -1.0 / HW)
@@ -46,7 +46,7 @@ def tile_cssrclassifier_pa_kernel(tc, d, W_dec, x, out_0, out_1, out_2):
 
         d_raw, d_grouped, d_codes, d_scales = {}, {}, {}, {}
         w_raw, w_bank, w_grouped, w_codes, w_scales = {}, {}, {}, {}, {}
-        x_raw, neg_x, neg_xt, recon = {}, {}, {}, {}
+        x_raw, neg_x, x_t, recon = {}, {}, {}, {}
 
         def bank():
             return psum.tile([P, BANK], F32, name="bank")
@@ -65,38 +65,31 @@ def tile_cssrclassifier_pa_kernel(tc, d, W_dec, x, out_0, out_1, out_2):
             nc.sync.dma_start(out=w_raw[k][:, slots], in_=src[:, slots])
 
         def load_x(h):
-            x_raw[h] = keep.tile([P, PAIR, PACK * HW], BF16, name="x_raw%d" % h)
+            x_raw[h] = keep.tile([P, PAIR, PACK, HW], BF16, name="x_raw%d" % h)
             nc.sync.dma_start(
-                out=x_raw[h][:],
+                out=x_raw[h][:].rearrange("p b t n -> p b (t n)"),
                 in_=x[PAIR * h : PAIR * (h + 1)].rearrange("b (m t) h w -> m b (t h w)", t=PACK),
             )
 
         def negate_x(h):
-            neg_x[h] = keep.tile([P, PAIR, PACK, HW], F32, name="neg_x%d" % h)
-            nc.vector.tensor_scalar_mul(
-                out=neg_x[h][:].rearrange("p b t n -> p (b t n)"),
-                in0=x_raw[h][:].rearrange("p b n -> p (b n)"),
-                scalar1=-1.0,
-            )
+            neg_x[h] = keep.tile([P, PACK, HW], F32, name="neg_x%d" % h)
+            nc.scalar.mul(out=neg_x[h][:], in_=x_raw[h][:, 0], mul=-1.0)
 
-        def patch(tile, q, t):
-            b, hh = divmod(q, 2)
-            return tile[:, b, t, hh * P : (hh + 1) * P]
-
-        def transpose_x(h, q):
-            acc = bank()
-            for t in range(PACK):
-                nc.tensor.transpose(acc[:, t * P : (t + 1) * P], patch(neg_x[h], q, t), ident[:])
-            neg_xt[h, q] = keep.tile([P, C], F32, name="neg_xt%d_%d" % (h, q))
-            nc.scalar.copy(out=neg_xt[h, q][:], in_=acc[:])
+        def transpose_x(h):
+            acc = psum.tile([P, 2, C], BF16, name="bank")
+            for hh in range(2):
+                for t in range(PACK):
+                    nc.tensor.transpose(
+                        acc[:, hh, t * P : (t + 1) * P], x_raw[h][:, 1, t, hh * P : (hh + 1) * P], ident_bf16[:]
+                    )
+            x_t[h] = keep.tile([P, 2, C], BF16, name="x_t%d" % h)
+            nc.vector.tensor_copy(out=x_t[h][:], in_=acc[:])
 
         def interleave_d(s, images=slice(0, PAIR)):
             if images.start == 0:
-                d_grouped[s] = work.tile([P, PAIR, HW, PACK], BF16, name="d_grouped", align_bytes=64)
-            nc.vector.tensor_copy(
-                out=d_grouped[s][:, images].rearrange("p b (c i) j -> p b c j i", i=4),
-                in_=d_raw[s][:, images].rearrange("p b j (c i) -> p b c j i", i=4),
-            )
+                d_grouped[s] = work.tile([P, PAIR, HW, PACK], BF16, name="d_grouped", align_bytes=64, bufs=1)
+            engine = nc.vector if s < 2 else nc.gpsimd
+            engine.tensor_copy(out=d_grouped[s][:, images], in_=d_raw[s][:, images].rearrange("p b j n -> p b n j"))
 
         def quantize_d(s):
             d_codes[s] = loads.tile([P, PAIR * HW], U32, name="d_codes", align_bytes=64)
@@ -175,13 +168,17 @@ def tile_cssrclassifier_pa_kernel(tc, d, W_dec, x, out_0, out_1, out_2):
                 accum_out=sums[:, h * PATCHES + q, k : k + 1],
             )
 
-        def difference_by_transposes(s, q):
-            h = s % 2
+        def difference_by_transposes(s, hh):
             acc = bank()
+            span = slice(hh * P, (hh + 1) * P)
             for t in range(PACK):
                 cols = acc[:, t * P : (t + 1) * P]
-                nc.tensor.matmul(cols, lhsT=patch(neg_x[h], q, t), rhs=ident[:], start=True, stop=False, is_transpose=True)
-                nc.tensor.matmul(cols, lhsT=patch(recon[s], q, t), rhs=ident[:], start=False, stop=True, is_transpose=True)
+                nc.tensor.matmul(
+                    cols, lhsT=neg_x[s % 2][:, t, span], rhs=ident[:], start=True, stop=False, is_transpose=True
+                )
+                nc.tensor.matmul(
+                    cols, lhsT=recon[s][:, 0, t, span], rhs=ident[:], start=False, stop=True, is_transpose=True
+                )
             return acc
 
         def store_recon(s):
@@ -191,12 +188,15 @@ def tile_cssrclassifier_pa_kernel(tc, d, W_dec, x, out_0, out_1, out_2):
                 in_=recon[s][:].rearrange("p b t n -> p b (t n)"),
             )
 
-        def vector_banks(s):
-            if s < 2:
-                return 0
+        def vector_slots(s):
             if s + 2 >= STEPS:
-                return PACK
-            return 1 + s % 2
+                return (1, 2, 3)
+            return (1, 3)
+
+        def weight_halves(s):
+            if s == 0 or s + 2 >= STEPS:
+                return ()
+            return (2, 3) if s == 1 else (s + 2,)
 
         load_w(0, slice(0, 2))
         load_d(0, slice(0, 1))
@@ -204,8 +204,8 @@ def tile_cssrclassifier_pa_kernel(tc, d, W_dec, x, out_0, out_1, out_2):
         load_w(0, slice(2, 4))
         load_d(1)
         load_x(0)
-        load_w(1)
         load_d(2)
+        load_w(1)
         load_x(1)
         load_d(3)
         load_d(4)
@@ -217,9 +217,8 @@ def tile_cssrclassifier_pa_kernel(tc, d, W_dec, x, out_0, out_1, out_2):
         copy_w(1, nc.scalar.copy)
         quantize_w(0)
         quantize_d(0)
-        quantize_w(1)
         interleave_d(1)
-        negate_x(0)
+        quantize_w(1)
         quantize_d(1)
 
         for s in range(STEPS + 1):
@@ -234,32 +233,43 @@ def tile_cssrclassifier_pa_kernel(tc, d, W_dec, x, out_0, out_1, out_2):
             if s < STEPS:
                 recon[s] = loads.tile([P, PAIR, PACK, HW], F32, name="recon", bufs=6)
                 accs = [decode(s, t) for t in range(PACK)]
-                direct = [decode_transposed(s, q) for q in BY_MATMUL]
-                if s == 0:
-                    transpose_w(2)
-                if s + 2 < STEPS:
-                    copy_w(s + 2, nc.vector.tensor_copy)
+                direct = [decode_transposed(s, 2 + hh) for hh in range(2)]
+                if s > 1:
+                    for i in weight_halves(s):
+                        copy_w(i, nc.vector.tensor_copy)
                 for t in range(PACK):
-                    engine_copy = nc.vector.tensor_copy if t >= PACK - vector_banks(s) else nc.scalar.copy
+                    engine_copy = nc.vector.tensor_copy if t in vector_slots(s) else nc.scalar.copy
                     engine_copy(out=recon[s][:, :, t, :], in_=accs[t][:].rearrange("p (b n) -> p b n", b=PAIR))
                 store_recon(s)
-                if s == 0:
-                    negate_x(1)
-                for q, acc in zip(BY_MATMUL, direct):
-                    if s < 2:
-                        transpose_x(h, q)
+                if s < 2:
+                    transpose_x(h)
+                    negate_x(h)
+                if s == 1:
+                    for i in weight_halves(s):
+                        transpose_w(i)
+                        copy_w(i, nc.scalar.copy)
+                for hh, acc in enumerate(direct):
                     diff = work.tile([P, C], F32, name="diff")
-                    nc.vector.tensor_tensor(out=diff[:], in0=acc[:], in1=neg_xt[h, q][:], op=ALU.add)
-                    diffs.append((q, diff))
+                    nc.vector.tensor_tensor(out=diff[:], in0=acc[:], in1=x_t[h][:, hh], op=ALU.subtract)
+                    diffs.append(diff)
+            for i in weight_halves(s):
+                quantize_w(i)
             if s + 2 < STEPS:
-                quantize_w(s + 2)
                 quantize_d(s + 2)
-            if s > 0:
-                for q in by_transpose:
-                    abs_sum(s - 1, q, difference_by_transposes(s - 1, q))
-            for q, diff in diffs:
-                abs_sum(s, q, diff)
-            if s + 3 < STEPS:
+            for hh in range(2):
+                if s > 0:
+                    abs_sum(s - 1, hh, difference_by_transposes(s - 1, hh))
+            if s == STEPS - 1:
+                plain = keep.tile([P, 2], F32, name="plain")
+                for hh, diff in enumerate(diffs):
+                    nc.vector.tensor_reduce(
+                        out=plain[:, hh : hh + 1], in_=diff[:], axis=AX.X, op=ALU.add, apply_absolute_value=True
+                    )
+                nc.vector.tensor_scalar_mul(out=sums[:, 2 * B - 2 :, K - 1], in0=plain[:], scalar1=-REDUCTION)
+            else:
+                for hh, diff in enumerate(diffs):
+                    abs_sum(s, 2 + hh, diff)
+            if 0 < s and s + 3 < STEPS:
                 transpose_w(s + 3)
 
         units = B * 2

@@ -22,6 +22,7 @@ PACK = 4
 BANK = 512
 PAIR = 2
 STEPS = K * B // PAIR
+SPLIT = 232
 PATCHES = PAIR * HW // P
 
 
@@ -88,8 +89,15 @@ def tile_cssrclassifier_pa_kernel(tc, d, W_dec, x, out_0, out_1, out_2):
         def interleave_d(s, images=slice(0, PAIR)):
             if images.start == 0:
                 d_grouped[s] = work.tile([P, PAIR, HW, PACK], BF16, name="d_grouped", align_bytes=64, bufs=1)
-            engine = nc.vector if s < 2 else nc.gpsimd
-            engine.tensor_copy(out=d_grouped[s][:, images], in_=d_raw[s][:, images].rearrange("p b j n -> p b n j"))
+            src = d_raw[s][:, images].rearrange("p b j n -> p b n j")
+            if s < 2:
+                nc.vector.tensor_copy(out=d_grouped[s][:, images], in_=src)
+            else:
+                nc.gpsimd.tensor_copy(out=d_grouped[s][:, :, :SPLIT], in_=src[:, :, :SPLIT])
+
+        def interleave_rest(s):
+            src = d_raw[s][:].rearrange("p b j n -> p b n j")
+            nc.scalar.copy(out=d_grouped[s][:, :, SPLIT:], in_=src[:, :, SPLIT:])
 
         def quantize_d(s):
             d_codes[s] = loads.tile([P, PAIR * HW], U32, name="d_codes", align_bytes=64)
@@ -191,7 +199,7 @@ def tile_cssrclassifier_pa_kernel(tc, d, W_dec, x, out_0, out_1, out_2):
         def vector_slots(s):
             if s + 2 >= STEPS:
                 return (1, 2, 3)
-            return (1, 3)
+            return () if s == 0 else (1, 3)
 
         def weight_halves(s):
             if s == 0 or s + 2 >= STEPS:
@@ -217,8 +225,8 @@ def tile_cssrclassifier_pa_kernel(tc, d, W_dec, x, out_0, out_1, out_2):
         copy_w(1, nc.scalar.copy)
         quantize_w(0)
         quantize_d(0)
-        interleave_d(1)
         quantize_w(1)
+        interleave_d(1)
         quantize_d(1)
 
         for s in range(STEPS + 1):
@@ -241,6 +249,8 @@ def tile_cssrclassifier_pa_kernel(tc, d, W_dec, x, out_0, out_1, out_2):
                     engine_copy = nc.vector.tensor_copy if t in vector_slots(s) else nc.scalar.copy
                     engine_copy(out=recon[s][:, :, t, :], in_=accs[t][:].rearrange("p (b n) -> p b n", b=PAIR))
                 store_recon(s)
+                if s + 2 < STEPS:
+                    interleave_rest(s + 2)
                 if s < 2:
                     transpose_x(h)
                     negate_x(h)

@@ -19,11 +19,16 @@ AX = mybir.AxisListType
 
 P = 128
 PACK = 4
+SLOTS = C // P
 BANK = 512
 PAIR = 2
+HALVES = HW // P
+PATCHES = PAIR * HALVES
 STEPS = K * B // PAIR
+W_PARTS = 2 * K
 SPLIT = 232
-PATCHES = PAIR * HW // P
+RECON_BUFS = 7
+QUADRANT = 32
 
 
 def tile_cssrclassifier_pa_kernel(tc, d, W_dec, x, out_0, out_1, out_2):
@@ -31,7 +36,7 @@ def tile_cssrclassifier_pa_kernel(tc, d, W_dec, x, out_0, out_1, out_2):
 
     with ExitStack() as ctx:
         keep = ctx.enter_context(tc.tile_pool(name="keep", bufs=1))
-        loads = ctx.enter_context(tc.tile_pool(name="loads", bufs=4))
+        deep = ctx.enter_context(tc.tile_pool(name="deep", bufs=4))
         work = ctx.enter_context(tc.tile_pool(name="work", bufs=3))
         psum = ctx.enter_context(tc.psum_pool(name="psum", bufs=8))
         ctx.enter_context(tc.manual_schedule())
@@ -43,7 +48,7 @@ def tile_cssrclassifier_pa_kernel(tc, d, W_dec, x, out_0, out_1, out_2):
         selector = keep.tile([P, P + B - 1], F32, name="selector")
         nc.gpsimd.memset(selector[:], 0.0)
         nc.gpsimd.memset(selector[:, B - 1 : B], -1.0 / HW)
-        sums = keep.tile([P, B * 2, K], F32, name="sums")
+        sums = keep.tile([P, B * HALVES, K], F32, name="sums")
 
         d_raw, d_grouped, d_codes, d_scales = {}, {}, {}, {}
         w_raw, w_bank, w_grouped, w_codes, w_scales = {}, {}, {}, {}, {}
@@ -52,56 +57,59 @@ def tile_cssrclassifier_pa_kernel(tc, d, W_dec, x, out_0, out_1, out_2):
         def bank():
             return psum.tile([P, BANK], F32, name="bank")
 
-        def load_d(s, images=slice(0, PAIR)):
-            k, h = divmod(s, 2)
+        def load_d(k, images=slice(0, B)):
             if images.start == 0:
-                d_raw[s] = loads.tile([P, PAIR, PACK, HW], BF16, name="d_raw", bufs=6)
-            src = d[k, PAIR * h : PAIR * (h + 1)].rearrange("b (p j) h w -> p b j (h w)", j=PACK)
-            nc.sync.dma_start(out=d_raw[s][:, images], in_=src[:, images])
+                d_raw[k] = keep.tile([P, B, PACK, HW], BF16, name="d_raw%d" % k)
+            src = d[k].rearrange("b (p j) h w -> p b j (h w)", j=PACK)
+            nc.sync.dma_start(out=d_raw[k][:, images], in_=src[:, images])
 
-        def load_w(k, slots=slice(0, PACK)):
+        def d_pair(s):
+            k, h = divmod(s, 2)
+            return d_raw[k][:, PAIR * h : PAIR * (h + 1)]
+
+        def load_w(k, slots=slice(0, SLOTS)):
             if slots.start == 0:
-                w_raw[k] = loads.tile([P, PACK, HID], BF16, name="w_raw")
-            src = W_dec[k].rearrange("(m t) j -> m t j", t=PACK)
+                w_raw[k] = keep.tile([P, SLOTS, HID], BF16, name="w_raw%d" % k)
+            src = W_dec[k].rearrange("(m t) j -> m t j", t=SLOTS)
             nc.sync.dma_start(out=w_raw[k][:, slots], in_=src[:, slots])
 
         def load_x(h):
-            x_raw[h] = keep.tile([P, PAIR, PACK, HW], BF16, name="x_raw%d" % h)
+            x_raw[h] = keep.tile([P, PAIR, SLOTS, HW], BF16, name="x_raw%d" % h)
             nc.sync.dma_start(
                 out=x_raw[h][:].rearrange("p b t n -> p b (t n)"),
-                in_=x[PAIR * h : PAIR * (h + 1)].rearrange("b (m t) h w -> m b (t h w)", t=PACK),
+                in_=x[PAIR * h : PAIR * (h + 1)].rearrange("b (m t) h w -> m b (t h w)", t=SLOTS),
             )
 
         def negate_x(h):
-            neg_x[h] = keep.tile([P, PACK, HW], F32, name="neg_x%d" % h)
+            neg_x[h] = keep.tile([P, SLOTS, HW], F32, name="neg_x%d" % h)
             nc.scalar.mul(out=neg_x[h][:], in_=x_raw[h][:, 0], mul=-1.0)
 
         def transpose_x(h):
-            acc = psum.tile([P, 2, C], BF16, name="bank")
-            for hh in range(2):
-                for t in range(PACK):
+            acc = psum.tile([P, HALVES, C], BF16, name="bank")
+            for half in range(HALVES):
+                for t in range(SLOTS):
                     nc.tensor.transpose(
-                        acc[:, hh, t * P : (t + 1) * P], x_raw[h][:, 1, t, hh * P : (hh + 1) * P], ident_bf16[:]
+                        acc[:, half, t * P : (t + 1) * P], x_raw[h][:, 1, t, half * P : (half + 1) * P], ident_bf16[:]
                     )
-            x_t[h] = keep.tile([P, 2, C], BF16, name="x_t%d" % h)
+            x_t[h] = keep.tile([P, HALVES, C], BF16, name="x_t%d" % h)
             nc.vector.tensor_copy(out=x_t[h][:], in_=acc[:])
 
         def interleave_d(s, images=slice(0, PAIR)):
             if images.start == 0:
                 d_grouped[s] = work.tile([P, PAIR, HW, PACK], BF16, name="d_grouped", align_bytes=64, bufs=1)
-            src = d_raw[s][:, images].rearrange("p b j n -> p b n j")
+            src = d_pair(s)[:, images].rearrange("p b j n -> p b n j")
             if s < 2:
                 nc.vector.tensor_copy(out=d_grouped[s][:, images], in_=src)
             else:
                 nc.gpsimd.tensor_copy(out=d_grouped[s][:, :, :SPLIT], in_=src[:, :, :SPLIT])
 
         def interleave_rest(s):
-            src = d_raw[s][:].rearrange("p b j n -> p b n j")
+            src = d_pair(s).rearrange("p b j n -> p b n j")
             nc.scalar.copy(out=d_grouped[s][:, :, SPLIT:], in_=src[:, :, SPLIT:])
 
         def quantize_d(s):
-            d_codes[s] = loads.tile([P, PAIR * HW], U32, name="d_codes", align_bytes=64)
-            d_scales[s] = loads.tile([P, PAIR * HW], U8, name="d_scales", align_bytes=64)
+            d_codes[s] = deep.tile([P, PAIR * HW], U32, name="d_codes", align_bytes=64)
+            d_scales[s] = deep.tile([P, PAIR * HW], U8, name="d_scales", align_bytes=64)
             nc.vector.quantize_mx(
                 out=d_codes[s][:].bitcast(E5M2X4),
                 scales=d_scales[s][:],
@@ -124,11 +132,11 @@ def tile_cssrclassifier_pa_kernel(tc, d, W_dec, x, out_0, out_1, out_2):
             )
 
         def quantize_w(i):
-            k, half = divmod(i, 2)
-            if half == 0:
+            k, part = divmod(i, 2)
+            if part == 0:
                 w_codes[k] = work.tile([P, C], U32, name="w_codes", align_bytes=64)
                 w_scales[k] = work.tile([P, C], U8, name="w_scales", align_bytes=64)
-            cols = slice(half * 2 * P, (half + 1) * 2 * P)
+            cols = slice(part * 2 * P, (part + 1) * 2 * P)
             nc.vector.quantize_mx(
                 out=w_codes[k][:, cols].bitcast(E5M2X4),
                 scales=w_scales[k][:, cols],
@@ -176,10 +184,10 @@ def tile_cssrclassifier_pa_kernel(tc, d, W_dec, x, out_0, out_1, out_2):
                 accum_out=sums[:, h * PATCHES + q, k : k + 1],
             )
 
-        def difference_by_transposes(s, hh):
+        def difference_by_transposes(s, half):
             acc = bank()
-            span = slice(hh * P, (hh + 1) * P)
-            for t in range(PACK):
+            span = slice(half * P, (half + 1) * P)
+            for t in range(SLOTS):
                 cols = acc[:, t * P : (t + 1) * P]
                 nc.tensor.matmul(
                     cols, lhsT=neg_x[s % 2][:, t, span], rhs=ident[:], start=True, stop=False, is_transpose=True
@@ -192,7 +200,7 @@ def tile_cssrclassifier_pa_kernel(tc, d, W_dec, x, out_0, out_1, out_2):
         def store_recon(s):
             k, h = divmod(s, 2)
             nc.sync.dma_start(
-                out=out_2[PAIR * h : PAIR * (h + 1), k].rearrange("b (m t) h w -> m b (t h w)", t=PACK),
+                out=out_2[PAIR * h : PAIR * (h + 1), k].rearrange("b (m t) h w -> m b (t h w)", t=SLOTS),
                 in_=recon[s][:].rearrange("p b t n -> p b (t n)"),
             )
 
@@ -201,8 +209,8 @@ def tile_cssrclassifier_pa_kernel(tc, d, W_dec, x, out_0, out_1, out_2):
                 return (1, 2, 3)
             return () if s == 0 else (1, 3)
 
-        def weight_halves(s):
-            if s == 0 or s + 2 >= STEPS:
+        def weight_parts(s):
+            if s == 0 or s + 2 >= W_PARTS:
                 return ()
             return (2, 3) if s == 1 else (s + 2,)
 
@@ -210,13 +218,12 @@ def tile_cssrclassifier_pa_kernel(tc, d, W_dec, x, out_0, out_1, out_2):
         load_d(0, slice(0, 1))
         load_d(0, slice(1, 2))
         load_w(0, slice(2, 4))
-        load_d(1)
+        load_d(0, slice(2, 4))
         load_x(0)
-        load_d(2)
+        load_d(1, slice(0, 2))
         load_w(1)
         load_x(1)
-        load_d(3)
-        load_d(4)
+        load_d(1, slice(2, 4))
         transpose_w(0)
         transpose_w(1)
         interleave_d(0, slice(0, 1))
@@ -231,21 +238,20 @@ def tile_cssrclassifier_pa_kernel(tc, d, W_dec, x, out_0, out_1, out_2):
 
         for s in range(STEPS + 1):
             h = s % 2
-            if h == 0 and s + 4 < STEPS:
-                load_w(s // 2 + 2)
-            if s + 5 < STEPS:
-                load_d(s + 5)
+            if s + 2 < K:
+                load_w(s + 2)
+                load_d(s + 2)
             if s + 2 < STEPS:
                 interleave_d(s + 2)
             diffs = []
             if s < STEPS:
-                recon[s] = loads.tile([P, PAIR, PACK, HW], F32, name="recon", bufs=6)
-                accs = [decode(s, t) for t in range(PACK)]
-                direct = [decode_transposed(s, 2 + hh) for hh in range(2)]
+                recon[s] = deep.tile([P, PAIR, SLOTS, HW], F32, name="recon", bufs=RECON_BUFS)
+                accs = [decode(s, t) for t in range(SLOTS)]
+                turned = [decode_transposed(s, HALVES + half) for half in range(HALVES)]
                 if s > 1:
-                    for i in weight_halves(s):
+                    for i in weight_parts(s):
                         copy_w(i, nc.vector.tensor_copy)
-                for t in range(PACK):
+                for t in range(SLOTS):
                     engine_copy = nc.vector.tensor_copy if t in vector_slots(s) else nc.scalar.copy
                     engine_copy(out=recon[s][:, :, t, :], in_=accs[t][:].rearrange("p (b n) -> p b n", b=PAIR))
                 store_recon(s)
@@ -255,75 +261,87 @@ def tile_cssrclassifier_pa_kernel(tc, d, W_dec, x, out_0, out_1, out_2):
                     transpose_x(h)
                     negate_x(h)
                 if s == 1:
-                    for i in weight_halves(s):
+                    for i in weight_parts(s):
                         transpose_w(i)
                         copy_w(i, nc.scalar.copy)
-                for hh, acc in enumerate(direct):
-                    diff = work.tile([P, C], F32, name="diff")
-                    nc.vector.tensor_tensor(out=diff[:], in0=acc[:], in1=x_t[h][:, hh], op=ALU.subtract)
+                for half, acc in enumerate(turned):
+                    diff = deep.tile([P, C], F32, name="diff")
+                    nc.vector.tensor_tensor(out=diff[:], in0=acc[:], in1=x_t[h][:, half], op=ALU.subtract)
                     diffs.append(diff)
-            for i in weight_halves(s):
+            for i in weight_parts(s):
                 quantize_w(i)
             if s + 2 < STEPS:
                 quantize_d(s + 2)
-            for hh in range(2):
-                if s > 0:
-                    abs_sum(s - 1, hh, difference_by_transposes(s - 1, hh))
+            if s > 0:
+                for half in range(HALVES):
+                    abs_sum(s - 1, half, difference_by_transposes(s - 1, half))
             if s == STEPS - 1:
-                plain = keep.tile([P, 2], F32, name="plain")
-                for hh, diff in enumerate(diffs):
+                unscaled = keep.tile([P, HALVES], F32, name="unscaled")
+                for half, diff in enumerate(diffs):
                     nc.vector.tensor_reduce(
-                        out=plain[:, hh : hh + 1], in_=diff[:], axis=AX.X, op=ALU.add, apply_absolute_value=True
+                        out=unscaled[:, half : half + 1], in_=diff[:], axis=AX.X, op=ALU.add, apply_absolute_value=True
                     )
-                nc.vector.tensor_scalar_mul(out=sums[:, 2 * B - 2 :, K - 1], in0=plain[:], scalar1=-REDUCTION)
+                nc.vector.tensor_scalar_mul(
+                    out=sums[:, (B - 1) * HALVES :, K - 1], in0=unscaled[:], scalar1=-REDUCTION
+                )
             else:
-                for hh, diff in enumerate(diffs):
-                    abs_sum(s, 2 + hh, diff)
-            if 0 < s and s + 3 < STEPS:
+                for half, diff in enumerate(diffs):
+                    abs_sum(s, HALVES + half, diff)
+            if 0 < s and s + 3 < W_PARTS:
                 transpose_w(s + 3)
 
-        units = B * 2
+        patches = B * HALVES
         both = keep.tile([P, P], F32, name="both")
-        logits = both[:, units * K :]
-        logits3 = logits.rearrange("p (u k) -> p u k", k=K)
+        clamped = both[:, patches * K :]
+        clamped_by_class = clamped.rearrange("p (q k) -> p q k", k=K)
         nc.vector.tensor_scalar(
-            out=logits, in0=sums[:].rearrange("p u k -> p (u k)"),
-            scalar1=-CLAMP, scalar2=CLAMP, op0=ALU.max, op1=ALU.min,
+            out=clamped,
+            in0=sums[:].rearrange("p q k -> p (q k)"),
+            scalar1=-CLAMP,
+            scalar2=CLAMP,
+            op0=ALU.max,
+            op1=ALU.min,
         )
-        top = keep.tile([P, units], F32, name="top")
-        nc.vector.tensor_reduce(out=top[:], in_=logits3, axis=AX.X, op=ALU.min)
-        shifted = keep.tile([P, units, K], F32, name="shifted")
+        least = keep.tile([P, patches], F32, name="least")
+        nc.vector.tensor_reduce(out=least[:], in_=clamped_by_class, axis=AX.X, op=ALU.min)
+        shifted = keep.tile([P, patches, K], F32, name="shifted")
         nc.vector.tensor_tensor(
-            out=shifted[:], in0=logits3, in1=top[:].unsqueeze(2).to_broadcast([P, units, K]), op=ALU.subtract
+            out=shifted[:],
+            in0=clamped_by_class,
+            in1=least[:].unsqueeze(2).to_broadcast([P, patches, K]),
+            op=ALU.subtract,
         )
         pooled = bank()
         for b in range(B):
             nc.tensor.matmul(
-                pooled[:, : 2 * K],
+                pooled[:, : HALVES * K],
                 lhsT=selector[:, B - 1 - b : B - 1 - b + P],
-                rhs=logits[:, b * 2 * K : (b + 1) * 2 * K],
+                rhs=clamped[:, b * HALVES * K : (b + 1) * HALVES * K],
                 start=(b == 0),
                 stop=(b == B - 1),
             )
-        powers = keep.tile([P, units, K], F32, name="powers")
+        powers = keep.tile([P, patches, K], F32, name="powers")
         nc.scalar.activation(out=powers[:], in_=shifted[:], func=ACT.Exp, scale=-1.0)
-        error = keep.tile([32, K], F32, name="error")
+        error = keep.tile([QUADRANT, K], F32, name="error")
         nc.vector.tensor_reduce(
-            out=error[:], in_=pooled[:32, : 2 * K].rearrange("p (h k) -> p k h", h=2), axis=AX.X, op=ALU.add
+            out=error[:],
+            in_=pooled[:QUADRANT, : HALVES * K].rearrange("p (g k) -> p k g", g=HALVES),
+            axis=AX.X,
+            op=ALU.add,
         )
         nc.sync.dma_start(out=out_1, in_=error[:B, :])
-        total = keep.tile([P, units], F32, name="total")
+        total = keep.tile([P, patches], F32, name="total")
         nc.vector.tensor_reduce(out=total[:], in_=powers[:], axis=AX.X, op=ALU.add)
-        inverse = keep.tile([P, units], F32, name="inverse")
+        inverse = keep.tile([P, patches], F32, name="inverse")
         nc.vector.reciprocal(out=inverse[:], in_=total[:])
         nc.vector.tensor_tensor(
-            out=both[:, : units * K].rearrange("p (b k h) -> p b h k", b=B, h=2),
-            in0=powers[:].rearrange("p (b h) k -> p b h k", h=2),
-            in1=inverse[:].rearrange("p (b h) -> p b h", h=2).unsqueeze(3).to_broadcast([P, B, 2, K]),
+            out=both[:, : patches * K].rearrange("p (b k g) -> p b g k", b=B, g=HALVES),
+            in0=powers[:].rearrange("p (b g) k -> p b g k", g=HALVES),
+            in1=inverse[:].rearrange("p (b g) -> p b g", g=HALVES).unsqueeze(3).to_broadcast([P, B, HALVES, K]),
             op=ALU.mult,
         )
         flipped = bank()
         nc.tensor.transpose(flipped[:, :P], both[:], ident[:])
-        rows = keep.tile([units * K, P], F32, name="rows")
-        nc.scalar.copy(out=rows[:], in_=flipped[: units * K, :P])
-        nc.sync.dma_start(out=out_0.rearrange("b k (g r) w -> (b k g) (r w)", g=2), in_=rows[:])
+        rows = keep.tile([patches * K, P], F32, name="rows")
+        nc.scalar.copy(out=rows[:], in_=flipped[: patches * K, :P])
+        nc.sync.dma_start(out=out_0.rearrange("b k (g r) w -> (b k g) (r w)", g=HALVES), in_=rows[:])

from contextlib import ExitStack

import concourse.mybir as mybir
from concourse.masks import make_identity

B, C, HW, K, HID = 4, 512, 256, 8, 512
REDUCTION = -0.1
CLAMP = 500.0
FLOPS = 2 * K * C * HID * B * HW

F32 = mybir.dt.float32
BF16 = mybir.dt.bfloat16
U32 = mybir.dt.uint32
U8 = mybir.dt.uint8
E5M2X4 = mybir.dt.float8_e5m2_x4
ALU = mybir.AluOpType
ACT = mybir.ActivationFunctionType
AX = mybir.AxisListType

P = 128
PACK = 4
SLOTS = C // P
BANK = 512
PAIR = 2
HALVES = HW // P
PATCHES = PAIR * HALVES
STEPS = K * B // PAIR
W_PARTS = 2 * K
SPLIT = 232
RECON_BUFS = 7
QUADRANT = 32


def tile_cssrclassifier_pa_kernel(tc, d, W_dec, x, out_0, out_1, out_2):
    nc = tc.nc

    with ExitStack() as ctx:
        keep = ctx.enter_context(tc.tile_pool(name="keep", bufs=1))
        deep = ctx.enter_context(tc.tile_pool(name="deep", bufs=4))
        work = ctx.enter_context(tc.tile_pool(name="work", bufs=3))
        psum = ctx.enter_context(tc.psum_pool(name="psum", bufs=8))
        ctx.enter_context(tc.manual_schedule())

        ident = keep.tile([P, P], F32, name="ident")
        make_identity(nc, ident[:])
        ident_bf16 = keep.tile([P, P], BF16, name="ident_bf16")
        make_identity(nc, ident_bf16[:])
        selector = keep.tile([P, P + B - 1], F32, name="selector")
        nc.gpsimd.memset(selector[:], 0.0)
        nc.gpsimd.memset(selector[:, B - 1 : B], -1.0 / HW)
        sums = keep.tile([P, B * HALVES, K], F32, name="sums")

        d_raw, d_grouped, d_codes, d_scales = {}, {}, {}, {}
        w_raw, w_bank, w_grouped, w_codes, w_scales = {}, {}, {}, {}, {}
        x_raw, neg_x, x_t, recon = {}, {}, {}, {}

        def bank():
            return psum.tile([P, BANK], F32, name="bank")

        def load_d(k, images=slice(0, B)):
            if images.start == 0:
                d_raw[k] = keep.tile([P, B, PACK, HW], BF16, name="d_raw%d" % k)
            src = d[k].rearrange("b (p j) h w -> p b j (h w)", j=PACK)
            nc.sync.dma_start(out=d_raw[k][:, images], in_=src[:, images])

        def d_pair(s):
            k, h = divmod(s, 2)
            return d_raw[k][:, PAIR * h : PAIR * (h + 1)]

        def load_w(k, slots=slice(0, SLOTS)):
            if slots.start == 0:
                w_raw[k] = keep.tile([P, SLOTS, HID], BF16, name="w_raw%d" % k)
            src = W_dec[k].rearrange("(m t) j -> m t j", t=SLOTS)
            nc.sync.dma_start(out=w_raw[k][:, slots], in_=src[:, slots])

        def load_x(h):
            x_raw[h] = keep.tile([P, PAIR, SLOTS, HW], BF16, name="x_raw%d" % h)
            nc.sync.dma_start(
                out=x_raw[h][:].rearrange("p b t n -> p b (t n)"),
                in_=x[PAIR * h : PAIR * (h + 1)].rearrange("b (m t) h w -> m b (t h w)", t=SLOTS),
            )

        def negate_x(h):
            neg_x[h] = keep.tile([P, SLOTS, HW], F32, name="neg_x%d" % h)
            nc.scalar.mul(out=neg_x[h][:], in_=x_raw[h][:, 0], mul=-1.0)

        def transpose_x(h):
            acc = psum.tile([P, HALVES, C], BF16, name="bank")
            for half in range(HALVES):
                for t in range(SLOTS):
                    nc.tensor.transpose(
                        acc[:, half, t * P : (t + 1) * P], x_raw[h][:, 1, t, half * P : (half + 1) * P], ident_bf16[:]
                    )
            x_t[h] = keep.tile([P, HALVES, C], BF16, name="x_t%d" % h)
            nc.vector.tensor_copy(out=x_t[h][:], in_=acc[:])

        def interleave_d(s, images=slice(0, PAIR)):
            if images.start == 0:
                d_grouped[s] = work.tile([P, PAIR, HW, PACK], BF16, name="d_grouped", align_bytes=64, bufs=1)
            src = d_pair(s)[:, images].rearrange("p b j n -> p b n j")
            if s < 2:
                nc.vector.tensor_copy(out=d_grouped[s][:, images], in_=src)
            else:
                nc.gpsimd.tensor_copy(out=d_grouped[s][:, :, :SPLIT], in_=src[:, :, :SPLIT])

        def interleave_rest(s):
            src = d_pair(s).rearrange("p b j n -> p b n j")
            nc.scalar.copy(out=d_grouped[s][:, :, SPLIT:], in_=src[:, :, SPLIT:])

        def quantize_d(s):
            d_codes[s] = deep.tile([P, PAIR * HW], U32, name="d_codes", align_bytes=64)
            d_scales[s] = deep.tile([P, PAIR * HW], U8, name="d_scales", align_bytes=64)
            nc.vector.quantize_mx(
                out=d_codes[s][:].bitcast(E5M2X4),
                scales=d_scales[s][:],
                in_=d_grouped[s][:].rearrange("p b n j -> p (b n j)"),
            )

        def transpose_w(i):
            w_bank[i] = bank()
            view = w_bank[i][:].rearrange("p (t u m) -> p t u m", t=2, u=2)
            for t in range(2):
                words = w_raw[i // 2][:, 2 * (i % 2) + t, :].bitcast(F32)
                for u in range(2):
                    nc.tensor.transpose(view[:, t, u, :], words[:, u : HID // 2 : 2], ident[:])

        def copy_w(i, engine_copy):
            w_grouped[i] = work.tile([P, 2 * P * PACK], BF16, name="w_grouped", align_bytes=64)
            engine_copy(
                out=w_grouped[i][:].bitcast(F32).rearrange("p (t m u) -> p t m u", t=2, u=2),
                in_=w_bank[i][:].rearrange("p (t u m) -> p t m u", t=2, u=2),
            )

        def quantize_w(i):
            k, part = divmod(i, 2)
            if part == 0:
                w_codes[k] = work.tile([P, C], U32, name="w_codes", align_bytes=64)
                w_scales[k] = work.tile([P, C], U8, name="w_scales", align_bytes=64)
            cols = slice(part * 2 * P, (part + 1) * 2 * P)
            nc.vector.quantize_mx(
                out=w_codes[k][:, cols].bitcast(E5M2X4),
                scales=w_scales[k][:, cols],
                in_=w_grouped[i][:],
            )

        def decode(s, t):
            k = s // 2
            acc = bank()
            cols = slice(t * P, (t + 1) * P)
            nc.tensor.matmul_mx(
                out=acc[:],
                lhsT=w_codes[k][:, cols].bitcast(E5M2X4),
                lhsT_scale=w_scales[k][:, cols],
                rhs=d_codes[s][:].bitcast(E5M2X4),
                rhs_scale=d_scales[s][:],
                start=True,
                stop=True,
            )
            return acc

        def decode_transposed(s, q):
            k = s // 2
            acc = bank()
            cols = slice(q * P, (q + 1) * P)
            nc.tensor.matmul_mx(
                out=acc[:],
                lhsT=d_codes[s][:, cols].bitcast(E5M2X4),
                lhsT_scale=d_scales[s][:, cols],
                rhs=w_codes[k][:].bitcast(E5M2X4),
                rhs_scale=w_scales[k][:],
                start=True,
                stop=True,
            )
            return acc

        def abs_sum(s, q, diff):
            k, h = divmod(s, 2)
            magnitude = work.tile([P, C], F32, name="magnitude")
            nc.scalar.activation(
                out=magnitude[:],
                in_=diff[:],
                func=ACT.Abs,
                scale=REDUCTION,
                accum_out=sums[:, h * PATCHES + q, k : k + 1],
            )

        def difference_by_transposes(s, half):
            acc = bank()
            span = slice(half * P, (half + 1) * P)
            for t in range(SLOTS):
                cols = acc[:, t * P : (t + 1) * P]
                nc.tensor.matmul(
                    cols, lhsT=neg_x[s % 2][:, t, span], rhs=ident[:], start=True, stop=False, is_transpose=True
                )
                nc.tensor.matmul(
                    cols, lhsT=recon[s][:, 0, t, span], rhs=ident[:], start=False, stop=True, is_transpose=True
                )
            return acc

        def store_recon(s):
            k, h = divmod(s, 2)
            nc.sync.dma_start(
                out=out_2[PAIR * h : PAIR * (h + 1), k].rearrange("b (m t) h w -> m b (t h w)", t=SLOTS),
                in_=recon[s][:].rearrange("p b t n -> p b (t n)"),
            )

        def vector_slots(s):
            if s + 2 >= STEPS:
                return (1, 2, 3)
            return () if s == 0 else (1, 3)

        def weight_parts(s):
            if s == 0 or s + 2 >= W_PARTS:
                return ()
            return (2, 3) if s == 1 else (s + 2,)

        load_w(0, slice(0, 2))
        load_d(0, slice(0, 1))
        load_d(0, slice(1, 2))
        load_w(0, slice(2, 4))
        load_d(0, slice(2, 4))
        load_x(0)
        load_d(1, slice(0, 2))
        load_w(1)
        load_x(1)
        load_d(1, slice(2, 4))
        transpose_w(0)
        transpose_w(1)
        interleave_d(0, slice(0, 1))
        interleave_d(0, slice(1, 2))
        copy_w(0, nc.scalar.copy)
        copy_w(1, nc.scalar.copy)
        quantize_w(0)
        quantize_d(0)
        quantize_w(1)
        interleave_d(1)
        quantize_d(1)

        for s in range(STEPS + 1):
            h = s % 2
            if s + 2 < K:
                load_w(s + 2)
                load_d(s + 2)
            if s + 2 < STEPS:
                interleave_d(s + 2)
            diffs = []
            if s < STEPS:
                recon[s] = deep.tile([P, PAIR, SLOTS, HW], F32, name="recon", bufs=RECON_BUFS)
                accs = [decode(s, t) for t in range(SLOTS)]
                turned = [decode_transposed(s, HALVES + half) for half in range(HALVES)]
                if s > 1:
                    for i in weight_parts(s):
                        copy_w(i, nc.vector.tensor_copy)
                for t in range(SLOTS):
                    engine_copy = nc.vector.tensor_copy if t in vector_slots(s) else nc.scalar.copy
                    engine_copy(out=recon[s][:, :, t, :], in_=accs[t][:].rearrange("p (b n) -> p b n", b=PAIR))
                store_recon(s)
                if s + 2 < STEPS:
                    interleave_rest(s + 2)
                if s < 2:
                    transpose_x(h)
                    negate_x(h)
                if s == 1:
                    for i in weight_parts(s):
                        transpose_w(i)
                        copy_w(i, nc.scalar.copy)
                for half, acc in enumerate(turned):
                    diff = deep.tile([P, C], F32, name="diff")
                    nc.vector.tensor_tensor(out=diff[:], in0=acc[:], in1=x_t[h][:, half], op=ALU.subtract)
                    diffs.append(diff)
            for i in weight_parts(s):
                quantize_w(i)
            if s + 2 < STEPS:
                quantize_d(s + 2)
            if s > 0:
                for half in range(HALVES):
                    abs_sum(s - 1, half, difference_by_transposes(s - 1, half))
            if s == STEPS - 1:
                unscaled = keep.tile([P, HALVES], F32, name="unscaled")
                for half, diff in enumerate(diffs):
                    nc.vector.tensor_reduce(
                        out=unscaled[:, half : half + 1], in_=diff[:], axis=AX.X, op=ALU.add, apply_absolute_value=True
                    )
                nc.vector.tensor_scalar_mul(
                    out=sums[:, (B - 1) * HALVES :, K - 1], in0=unscaled[:], scalar1=-REDUCTION
                )
            else:
                for half, diff in enumerate(diffs):
                    abs_sum(s, HALVES + half, diff)
            if 0 < s and s + 3 < W_PARTS:
                transpose_w(s + 3)

        patches = B * HALVES
        both = keep.tile([P, P], F32, name="both")
        clamped = both[:, patches * K :]
        clamped_by_class = clamped.rearrange("p (q k) -> p q k", k=K)
        nc.vector.tensor_scalar(
            out=clamped,
            in0=sums[:].rearrange("p q k -> p (q k)"),
            scalar1=-CLAMP,
            scalar2=CLAMP,
            op0=ALU.max,
            op1=ALU.min,
        )
        least = keep.tile([P, patches], F32, name="least")
        nc.vector.tensor_reduce(out=least[:], in_=clamped_by_class, axis=AX.X, op=ALU.min)
        shifted = keep.tile([P, patches, K], F32, name="shifted")
        nc.vector.tensor_tensor(
            out=shifted[:],
            in0=clamped_by_class,
            in1=least[:].unsqueeze(2).to_broadcast([P, patches, K]),
            op=ALU.subtract,
        )
        pooled = bank()
        for b in range(B):
            nc.tensor.matmul(
                pooled[:, : HALVES * K],
                lhsT=selector[:, B - 1 - b : B - 1 - b + P],
                rhs=clamped[:, b * HALVES * K : (b + 1) * HALVES * K],
                start=(b == 0),
                stop=(b == B - 1),
            )
        powers = keep.tile([P, patches, K], F32, name="powers")
        nc.scalar.activation(out=powers[:], in_=shifted[:], func=ACT.Exp, scale=-1.0)
        error = keep.tile([QUADRANT, K], F32, name="error")
        nc.vector.tensor_reduce(
            out=error[:],
            in_=pooled[:QUADRANT, : HALVES * K].rearrange("p (g k) -> p k g", g=HALVES),
            axis=AX.X,
            op=ALU.add,
        )
        nc.sync.dma_start(out=out_1, in_=error[:B, :])
        total = keep.tile([P, patches], F32, name="total")
        nc.vector.tensor_reduce(out=total[:], in_=powers[:], axis=AX.X, op=ALU.add)
        inverse = keep.tile([P, patches], F32, name="inverse")
        nc.vector.reciprocal(out=inverse[:], in_=total[:])
        nc.vector.tensor_tensor(
            out=both[:, : patches * K].rearrange("p (b k g) -> p b g k", b=B, g=HALVES),
            in0=powers[:].rearrange("p (b g) k -> p b g k", g=HALVES),
            in1=inverse[:].rearrange("p (b g) -> p b g", g=HALVES).unsqueeze(3).to_broadcast([P, B, HALVES, K]),
            op=ALU.mult,
        )
        flipped = bank()
        nc.tensor.transpose(flipped[:, :P], both[:], ident[:])
        rows = keep.tile([patches * K, P], F32, name="rows")
        nc.scalar.copy(out=rows[:], in_=flipped[: patches * K, :P])
        nc.sync.dma_start(out=out_0.rearrange("b k (g r) w -> (b k g) (r w)", g=HALVES), in_=rows[:])
